import numpy as np
import ml_dtypes


def mxq(x, axis, fmt="e4m3"):
    dtype, down = {"e4m3": (ml_dtypes.float8_e4m3fn, 7), "e5m2": (ml_dtypes.float8_e5m2, 14)}[fmt]
    v = np.moveaxis(np.asarray(x, np.float32).astype(ml_dtypes.bfloat16).astype(np.float64), axis, -1)
    blocks = v.reshape(v.shape[:-1] + (-1, 32))
    amax = np.abs(blocks).max(-1, keepdims=True)
    byte = np.maximum(np.where(amax > 0, np.frexp(amax)[1] - 1 + 127, 0) - down, 1)
    scale = np.exp2(byte - 127.0)
    codes = (blocks / scale).astype(np.float32).astype(dtype).astype(np.float64)
    return np.moveaxis((codes * scale).reshape(v.shape), -1, axis)


WIDE = False


def mx_kscale(k):
    if not WIDE:
        return np.ones(k)
    levels = np.array([10, -10, 5, -5, 0])
    if k % 512:
        return np.exp2(np.random.permutation(np.resize(levels, k // 32))).repeat(32)
    a = np.empty((k // 512, 16))
    for p in range(k // 512):
        a[p, :8] = np.random.permutation(np.resize(levels, 8))
        for g in range(8):
            far = levels[np.abs(levels - a[p, g]) >= 10]
            a[p, g + 8] = far[np.random.randint(len(far))]
    return np.exp2(a.ravel()).repeat(32)


BF16 = ml_dtypes.bfloat16


def bf(x):
    return np.asarray(x, np.float32).astype(BF16)


def f64(x):
    return np.asarray(x).astype(np.float64)


B, C, D, O = 2, 256, 2048, 128
S0 = 1
S = 2
P = D // (S * (S0 + 1))
K = S * C


def setup_inputs():
    s = mx_kscale(K).reshape(S, C)
    sx = np.tile(np.repeat(s.T, S0 + 1, axis=1), (1, P))
    return {"x": bf(np.random.standard_normal((B, C, D)) * sx),
            "weight": bf(np.random.standard_normal((O, C, 1, S)) / C ** 0.25 / s.T[None, :, None, :])}


def reference(x, weight):
    xp = f64(x).reshape(B, C, D // (S0 + 1), S0 + 1).sum(axis=-1)
    xr = xp.reshape(B, C, P, S)
    a = xr.transpose(0, 2, 3, 1).reshape(B, P, K)
    w = f64(weight)[:, :, 0, :].transpose(2, 1, 0).reshape(K, O)
    out = (mxq(a, 2, "e4m3") @ mxq(w, 0, "e4m3")) / np.sqrt(C)
    return out.transpose(0, 2, 1)

@@ -1,0 +1,154 @@
+from contextlib import ExitStack
+
+import concourse.mybir as mybir
+from concourse.masks import make_identity
+
+BF16 = mybir.dt.bfloat16
+F32 = mybir.dt.float32
+U32 = mybir.dt.uint32
+U8 = mybir.dt.uint8
+FP8X4 = mybir.dt.float8_e4m3fn_x4
+
+B, C, D, O = 2, 256, 2048, 128
+TAPS = 2
+PAIR = 2
+SPAN = TAPS * PAIR
+POSITIONS = D // SPAN
+PARTS = 128
+PACK = 4
+HALF = C // PACK
+BLOCK = 128
+BLOCKS = POSITIONS // BLOCK
+FLOPS = 2 * B * O * POSITIONS * C * TAPS
+
+
+def tile_nonoverlappingconv1d_shared_s_kernel(tc, x, weight, out):
+    nc = tc.nc
+    loads = [(0, 0, 64), (0, 64, 64), (1, 0, 128), (2, 0, 128), (3, 0, 128)]
+
+    with ExitStack() as ctx:
+        ctx.enter_context(tc.manual_schedule())
+        keep = ctx.enter_context(tc.tile_pool(name="keep", bufs=1))
+        stream = ctx.enter_context(tc.tile_pool(name="stream", bufs=BLOCKS))
+        raw_pool = ctx.enter_context(tc.tile_pool(name="raw_pool", bufs=len(loads)))
+        psum_w = ctx.enter_context(tc.psum_pool(name="psum_w", bufs=1))
+        psum_acc = ctx.enter_context(tc.psum_pool(name="psum_acc", bufs=BLOCKS - 1))
+        psum_last = ctx.enter_context(tc.psum_pool(name="psum_last", bufs=B))
+
+        w_rows = keep.tile([O, B, C * TAPS], BF16)
+        w_hbm = weight.rearrange("o c one k -> o (c one k)")
+        for b in range(B):
+            nc.scalar.dma_start(out=w_rows[:, b, :], in_=w_hbm)
+
+        x_rows = x.rearrange("b (q t) d -> (b q) t d", t=PACK)
+        raws = []
+        for block, first, n in loads:
+            start = (block * BLOCK + first) * SPAN
+            raw = raw_pool.tile([PARTS, PACK, n * SPAN], BF16, name="raw")
+            nc.sync.dma_start(out=raw[:], in_=x_rows[:, :, start : start + n * SPAN])
+            raws.append(raw)
+
+        w_grouped = keep.tile([PARTS, B, TAPS * O * PACK], BF16, align_bytes=64)
+        nc.vector.memset(w_grouped[:].rearrange("q b j -> q (b j)").bitcast(U32), 0)
+        identity = keep.tile([PARTS, PARTS], F32)
+        make_identity(nc, identity[:])
+        w_words = w_rows[:].rearrange("o b j -> o (b j)").bitcast(F32)
+        w_turned = psum_w.tile([PARTS, PACK, O], F32)
+        for t in range(PACK):
+            nc.tensor.transpose(w_turned[:, t, :], w_words[:, t : B * C : PACK], identity[:])
+        w_pairs = w_turned[:].rearrange("q t o -> q (t o)").bitcast(BF16)
+        w_pairs = w_pairs.rearrange("q (t o k) -> q k o t", t=PACK, k=TAPS)
+        for b in range(B):
+            rows = slice(b * HALF, (b + 1) * HALF)
+            nc.scalar.copy(
+                out=w_grouped[rows, b, :].rearrange("q (k o t) -> q k o t", k=TAPS, t=PACK),
+                in_=w_pairs[rows],
+            )
+        w_codes = keep.tile([PARTS, B, TAPS, O], U32, align_bytes=64)
+        w_scales = keep.tile([PARTS, B, TAPS, O], U8, align_bytes=64)
+
+        grouped = []
+        codes = []
+        scales = []
+        for block in range(BLOCKS):
+            x_grouped = stream.tile([PARTS, TAPS, BLOCK * PACK], BF16, align_bytes=64, name="x_grouped")
+            x_codes = stream.tile([PARTS, TAPS, BLOCK], U32, align_bytes=64, name="x_codes")
+            x_scales = stream.tile([PARTS, TAPS, BLOCK], U8, align_bytes=64, name="x_scales")
+            grouped.append(x_grouped)
+            codes.append(x_codes)
+            scales.append(x_scales)
+
+        def sum_pairs(i, taps):
+            block, first, n = loads[i]
+            pairs = raws[i][:].rearrange("q t (p k s) -> q k p t s", k=TAPS, s=PAIR)
+            target = grouped[block][:].rearrange("q k (p t) -> q k p t", t=PACK)
+            nc.vector.tensor_tensor(
+                out=target[:, taps, first : first + n, :],
+                in0=pairs[:, taps, :, :, 0],
+                in1=pairs[:, taps, :, :, 1],
+                op=mybir.AluOpType.add,
+            )
+
+        def quantise(block, taps):
+            nc.vector.quantize_mx(
+                out=codes[block][:, taps, :].rearrange("q k p -> q (k p)").bitcast(FP8X4),
+                scales=scales[block][:, taps, :].rearrange("q k p -> q (k p)"),
+                in_=grouped[block][:, taps, :].rearrange("q k j -> q (k j)"),
+            )
+
+        both = slice(0, TAPS)
+        sum_pairs(0, both)
+        sum_pairs(1, both)
+        sum_pairs(2, both)
+        quantise(0, both)
+        sum_pairs(3, both)
+        quantise(1, both)
+        nc.vector.quantize_mx(
+            out=w_codes[:].rearrange("q b k o -> q (b k o)").bitcast(FP8X4),
+            scales=w_scales[:].rearrange("q b k o -> q (b k o)"),
+            in_=w_grouped[:].rearrange("q b j -> q (b j)"),
+        )
+        sum_pairs(4, slice(0, 1))
+        quantise(2, both)
+        sum_pairs(4, slice(1, 2))
+        quantise(3, slice(0, 1))
+        quantise(3, slice(1, 2))
+
+        def multiply(acc, block, b, k):
+            nc.tensor.matmul_mx(
+                out=acc,
+                lhsT=w_codes[:, b, k, :].bitcast(FP8X4),
+                lhsT_scale=w_scales[:, b, k, :],
+                rhs=codes[block][:, k, :].bitcast(FP8X4),
+                rhs_scale=scales[block][:, k, :],
+                start=(k == 0),
+                stop=(k == TAPS - 1),
+            )
+
+        out_rows = out.rearrange("b o p -> o b p")
+        for block in range(BLOCKS - 1):
+            acc = psum_acc.tile([O, B, BLOCK], F32, name="acc")
+            for b in range(B):
+                for k in range(TAPS):
+                    multiply(acc[:, b, :], block, b, k)
+            result = stream.tile([O, B, BLOCK], F32, name="result")
+            nc.scalar.mul(out=result[:], in_=acc[:], mul=1.0 / 16.0)
+            nc.sync.dma_start(
+                out=out_rows[:, :, block * BLOCK : (block + 1) * BLOCK], in_=result[:]
+            )
+
+        last = BLOCKS - 1
+        accs = []
+        for b in range(B):
+            acc_last = psum_last.tile([O, BLOCK], F32, name="acc_last")
+            accs.append(acc_last)
+        for k in range(TAPS):
+            for b in range(B):
+                multiply(accs[b][:], last, b, k)
+        columns = slice(last * BLOCK, (last + 1) * BLOCK)
+        result0 = keep.tile([O, BLOCK], F32)
+        nc.scalar.mul(out=result0[:], in_=accs[0][:], mul=1.0 / 16.0)
+        nc.sync.dma_start(out=out[0, :, columns], in_=result0[:])
+        result1 = keep.tile([O, BLOCK], F32)
+        nc.vector.tensor_scalar_mul(result1[:], accs[1][:], 1.0 / 16.0)
+        nc.scalar.dma_start(out=out[1, :, columns], in_=result1[:])

@@ -17,6 +17,7 @@ POSITIONS = D // SPAN
 PARTS = 128
 PACK = 4
 HALF = C // PACK
+NEAR = 2
 BLOCK = 128
 BLOCKS = POSITIONS // BLOCK
 FLOPS = 2 * B * O * POSITIONS * C * TAPS
@@ -80,23 +81,25 @@ def tile_nonoverlappingconv1d_shared_s_kernel(tc, x, weight, out):
 
         def sum_pairs(i, taps):
             block, first, n = loads[i]
-            pairs = raws[i][:].rearrange("q t (p k s) -> q k p t s", k=TAPS, s=PAIR)
-            target = grouped[block][:].rearrange("q k (p t) -> q k p t", t=PACK)
-            nc.vector.tensor_tensor(
-                out=target[:, taps, first : first + n, :],
-                in0=pairs[:, taps, :, :, 0],
-                in1=pairs[:, taps, :, :, 1],
-                op=mybir.AluOpType.add,
-            )
+            pairs = raws[i][:].rearrange("q t (g h k s) -> q k g t h s", h=NEAR, k=TAPS, s=PAIR)
+            for k in taps:
+                target = grouped[block][:, k, first * PACK : (first + n) * PACK]
+                nc.vector.tensor_tensor(
+                    out=target.rearrange("q (g h t) -> q g t h", h=NEAR, t=PACK),
+                    in0=pairs[:, k, :, :, :, 0],
+                    in1=pairs[:, k, :, :, :, 1],
+                    op=mybir.AluOpType.add,
+                )
 
         def quantise(block, taps):
+            taps = slice(taps[0], taps[-1] + 1)
             nc.vector.quantize_mx(
                 out=codes[block][:, taps, :].rearrange("q k p -> q (k p)").bitcast(FP8X4),
                 scales=scales[block][:, taps, :].rearrange("q k p -> q (k p)"),
                 in_=grouped[block][:, taps, :].rearrange("q k j -> q (k j)"),
             )
 
-        both = slice(0, TAPS)
+        both = range(TAPS)
         sum_pairs(0, both)
         sum_pairs(1, both)
         sum_pairs(2, both)
@@ -108,11 +111,11 @@ def tile_nonoverlappingconv1d_shared_s_kernel(tc, x, weight, out):
             scales=w_scales[:].rearrange("q b k o -> q (b k o)"),
             in_=w_grouped[:].rearrange("q b j -> q (b j)"),
         )
-        sum_pairs(4, slice(0, 1))
+        sum_pairs(4, range(0, 1))
         quantise(2, both)
-        sum_pairs(4, slice(1, 2))
-        quantise(3, slice(0, 1))
-        quantise(3, slice(1, 2))
+        sum_pairs(4, range(1, 2))
+        quantise(3, range(0, 1))
+        quantise(3, range(1, 2))
 
         def multiply(acc, block, b, k):
             nc.tensor.matmul_mx(

@@ -25,32 +25,28 @@ FLOPS = 2 * B * O * POSITIONS * C * TAPS
 
 def tile_nonoverlappingconv1d_shared_s_kernel(tc, x, weight, out):
     nc = tc.nc
-    loads = [(0, 0, 64), (0, 64, 64), (1, 0, 128), (2, 0, 128), (3, 0, 128)]
 
     with ExitStack() as ctx:
         ctx.enter_context(tc.manual_schedule())
         keep = ctx.enter_context(tc.tile_pool(name="keep", bufs=1))
         stream = ctx.enter_context(tc.tile_pool(name="stream", bufs=BLOCKS))
-        raw_pool = ctx.enter_context(tc.tile_pool(name="raw_pool", bufs=len(loads)))
         psum_w = ctx.enter_context(tc.psum_pool(name="psum_w", bufs=1))
         psum_acc = ctx.enter_context(tc.psum_pool(name="psum_acc", bufs=BLOCKS - 1))
         psum_last = ctx.enter_context(tc.psum_pool(name="psum_last", bufs=B))
 
         w_rows = keep.tile([O, B, C * TAPS], BF16)
         w_hbm = weight.rearrange("o c one k -> o (c one k)")
-        for b in range(B):
-            nc.scalar.dma_start(out=w_rows[:, b, :], in_=w_hbm)
-
         x_rows = x.rearrange("b (q t) d -> (b q) t d", t=PACK)
         raws = []
-        for block, first, n in loads:
-            start = (block * BLOCK + first) * SPAN
-            raw = raw_pool.tile([PARTS, PACK, n * SPAN], BF16, name="raw")
-            nc.sync.dma_start(out=raw[:], in_=x_rows[:, :, start : start + n * SPAN])
+        for block in range(BLOCKS):
+            start = block * BLOCK * SPAN
+            raw = stream.tile([PARTS, PACK, BLOCK * SPAN], BF16, name="raw")
+            nc.sync.dma_start(out=raw[:], in_=x_rows[:, :, start : start + BLOCK * SPAN])
             raws.append(raw)
+            if block == 0:
+                nc.sync.dma_start(out=w_rows[:, 0, :], in_=w_hbm)
 
-        w_grouped = keep.tile([PARTS, B, TAPS * O * PACK], BF16, align_bytes=64)
-        nc.vector.memset(w_grouped[:].rearrange("q b j -> q (b j)").bitcast(U32), 0)
+        nc.scalar.copy(out=w_rows[:, 1, :], in_=w_rows[:, 0, :])
         identity = keep.tile([PARTS, PARTS], F32)
         make_identity(nc, identity[:])
         w_words = w_rows[:].rearrange("o b j -> o (b j)").bitcast(F32)
@@ -59,14 +55,26 @@ def tile_nonoverlappingconv1d_shared_s_kernel(tc, x, weight, out):
             nc.tensor.transpose(w_turned[:, t, :], w_words[:, t : B * C : PACK], identity[:])
         w_pairs = w_turned[:].rearrange("q t o -> q (t o)").bitcast(BF16)
         w_pairs = w_pairs.rearrange("q (t o k) -> q k o t", t=PACK, k=TAPS)
+        w_grouped = keep.tile([PARTS, TAPS * O * PACK], BF16, align_bytes=64)
+        nc.scalar.copy(
+            out=w_grouped[:].rearrange("q (k o t) -> q k o t", k=TAPS, t=PACK), in_=w_pairs
+        )
+        w_codes = []
+        w_scales = []
         for b in range(B):
-            rows = slice(b * HALF, (b + 1) * HALF)
-            nc.scalar.copy(
-                out=w_grouped[rows, b, :].rearrange("q (k o t) -> q k o t", k=TAPS, t=PACK),
-                in_=w_pairs[rows],
+            w_code = keep.tile([PARTS, TAPS, O], U32, align_bytes=64, name=f"w_codes{b}")
+            w_scale = keep.tile([PARTS, TAPS, O], U8, align_bytes=64, name=f"w_scales{b}")
+            w_codes.append(w_code)
+            w_scales.append(w_scale)
+
+        def quantise_weight(b):
+            nc.vector.quantize_mx(
+                out=w_codes[b][:].rearrange("q k o -> q (k o)").bitcast(FP8X4),
+                scales=w_scales[b][:].rearrange("q k o -> q (k o)"),
+                in_=w_grouped[:],
             )
-        w_codes = keep.tile([PARTS, B, TAPS, O], U32, align_bytes=64)
-        w_scales = keep.tile([PARTS, B, TAPS, O], U8, align_bytes=64)
+            other = 1 - b
+            nc.gpsimd.memset(w_codes[b][other * HALF : (other + 1) * HALF], 0)
 
         grouped = []
         codes = []
@@ -79,11 +87,10 @@ def tile_nonoverlappingconv1d_shared_s_kernel(tc, x, weight, out):
             codes.append(x_codes)
             scales.append(x_scales)
 
-        def sum_pairs(i, taps):
-            block, first, n = loads[i]
-            pairs = raws[i][:].rearrange("q t (g h k s) -> q k g t h s", h=NEAR, k=TAPS, s=PAIR)
+        def sum_pairs(block, taps):
+            pairs = raws[block][:].rearrange("q t (g h k s) -> q k g t h s", h=NEAR, k=TAPS, s=PAIR)
             for k in taps:
-                target = grouped[block][:, k, first * PACK : (first + n) * PACK]
+                target = grouped[block][:, k, :]
                 nc.vector.tensor_tensor(
                     out=target.rearrange("q (g h t) -> q g t h", h=NEAR, t=PACK),
                     in0=pairs[:, k, :, :, :, 0],
@@ -102,26 +109,23 @@ def tile_nonoverlappingconv1d_shared_s_kernel(tc, x, weight, out):
         both = range(TAPS)
         sum_pairs(0, both)
         sum_pairs(1, both)
-        sum_pairs(2, both)
         quantise(0, both)
-        sum_pairs(3, both)
+        sum_pairs(2, range(0, 1))
+        for b in range(B):
+            quantise_weight(b)
+        sum_pairs(2, range(1, 2))
         quantise(1, both)
-        nc.vector.quantize_mx(
-            out=w_codes[:].rearrange("q b k o -> q (b k o)").bitcast(FP8X4),
-            scales=w_scales[:].rearrange("q b k o -> q (b k o)"),
-            in_=w_grouped[:].rearrange("q b j -> q (b j)"),
-        )
-        sum_pairs(4, range(0, 1))
+        sum_pairs(3, range(0, 1))
         quantise(2, both)
-        sum_pairs(4, range(1, 2))
+        sum_pairs(3, range(1, 2))
         quantise(3, range(0, 1))
         quantise(3, range(1, 2))
 
         def multiply(acc, block, b, k):
             nc.tensor.matmul_mx(
                 out=acc,
-                lhsT=w_codes[:, b, k, :].bitcast(FP8X4),
-                lhsT_scale=w_scales[:, b, k, :],
+                lhsT=w_codes[b][:, k, :].bitcast(FP8X4),
+                lhsT_scale=w_scales[b][:, k, :],
                 rhs=codes[block][:, k, :].bitcast(FP8X4),
                 rhs_scale=scales[block][:, k, :],
                 start=(k == 0),

@@ -17,7 +17,6 @@ POSITIONS = D // SPAN
 PARTS = 128
 PACK = 4
 HALF = C // PACK
-NEAR = 2
 BLOCK = 128
 BLOCKS = POSITIONS // BLOCK
 FLOPS = 2 * B * O * POSITIONS * C * TAPS
@@ -87,16 +86,15 @@ def tile_nonoverlappingconv1d_shared_s_kernel(tc, x, weight, out):
             codes.append(x_codes)
             scales.append(x_scales)
 
-        def sum_pairs(block, taps):
-            pairs = raws[block][:].rearrange("q t (g h k s) -> q k g t h s", h=NEAR, k=TAPS, s=PAIR)
-            for k in taps:
-                target = grouped[block][:, k, :]
-                nc.vector.tensor_tensor(
-                    out=target.rearrange("q (g h t) -> q g t h", h=NEAR, t=PACK),
-                    in0=pairs[:, k, :, :, :, 0],
-                    in1=pairs[:, k, :, :, :, 1],
-                    op=mybir.AluOpType.add,
-                )
+        def sum_pairs(block, first, n):
+            pairs = raws[block][:].rearrange("q t (p k s) -> q p t k s", k=TAPS, s=PAIR)
+            target = grouped[block][:].rearrange("q k (p t) -> q p t k", t=PACK)
+            nc.vector.tensor_tensor(
+                out=target[:, first : first + n],
+                in0=pairs[:, first : first + n, :, :, 0],
+                in1=pairs[:, first : first + n, :, :, 1],
+                op=mybir.AluOpType.add,
+            )
 
         def quantise(block, taps):
             taps = slice(taps[0], taps[-1] + 1)
@@ -107,17 +105,17 @@ def tile_nonoverlappingconv1d_shared_s_kernel(tc, x, weight, out):
             )
 
         both = range(TAPS)
-        sum_pairs(0, both)
-        sum_pairs(1, both)
+        sum_pairs(0, 0, BLOCK)
+        sum_pairs(1, 0, BLOCK)
         quantise(0, both)
-        sum_pairs(2, range(0, 1))
+        sum_pairs(2, 0, BLOCK // 2)
         for b in range(B):
             quantise_weight(b)
-        sum_pairs(2, range(1, 2))
+        sum_pairs(2, BLOCK // 2, BLOCK // 2)
         quantise(1, both)
-        sum_pairs(3, range(0, 1))
+        sum_pairs(3, 0, BLOCK // 2)
         quantise(2, both)
-        sum_pairs(3, range(1, 2))
+        sum_pairs(3, BLOCK // 2, BLOCK // 2)
         quantise(3, range(0, 1))
         quantise(3, range(1, 2))
 

@@ -96,6 +96,24 @@ def tile_nonoverlappingconv1d_shared_s_kernel(tc, x, weight, out):
                 op=mybir.AluOpType.add,
             )
 
+        def split_words(block, first, n):
+            values = raws[block][:].rearrange("q t (p j) -> q p t j", j=SPAN)
+            apart = stream.tile([PARTS, SPAN, n * PACK], BF16, name="apart")
+            nc.scalar.copy(
+                out=apart[:].rearrange("q j (p t) -> q p t j", t=PACK),
+                in_=values[:, first : first + n],
+            )
+            return apart
+
+        def sum_apart(block, first, n, apart):
+            pairs = apart[:].rearrange("q (k s) m -> q k s m", s=PAIR)
+            nc.vector.tensor_tensor(
+                out=grouped[block][:, :, first * PACK : (first + n) * PACK],
+                in0=pairs[:, :, 0, :],
+                in1=pairs[:, :, 1, :],
+                op=mybir.AluOpType.add,
+            )
+
         def quantise(block, taps):
             taps = slice(taps[0], taps[-1] + 1)
             nc.vector.quantize_mx(
@@ -105,17 +123,21 @@ def tile_nonoverlappingconv1d_shared_s_kernel(tc, x, weight, out):
             )
 
         both = range(TAPS)
+        half = BLOCK // 2
+        apart2 = split_words(2, half, half)
+        apart3 = split_words(3, half, half)
         sum_pairs(0, 0, BLOCK)
         sum_pairs(1, 0, BLOCK)
         quantise(0, both)
-        sum_pairs(2, 0, BLOCK // 2)
+        sum_pairs(2, 0, half)
+        quantise(1, both)
         for b in range(B):
             quantise_weight(b)
-        sum_pairs(2, BLOCK // 2, BLOCK // 2)
-        quantise(1, both)
-        sum_pairs(3, 0, BLOCK // 2)
-        quantise(2, both)
-        sum_pairs(3, BLOCK // 2, BLOCK // 2)
+        sum_apart(2, half, half, apart2)
+        sum_pairs(3, 0, half)
+        quantise(2, range(0, 1))
+        sum_apart(3, half, half, apart3)
+        quantise(2, range(1, 2))
         quantise(3, range(0, 1))
         quantise(3, range(1, 2))
 

@@ -29,6 +29,7 @@ def tile_nonoverlappingconv1d_shared_s_kernel(tc, x, weight, out):
         ctx.enter_context(tc.manual_schedule())
         keep = ctx.enter_context(tc.tile_pool(name="keep", bufs=1))
         stream = ctx.enter_context(tc.tile_pool(name="stream", bufs=BLOCKS))
+        raw_pool = ctx.enter_context(tc.tile_pool(name="raw_pool", bufs=5))
         psum_w = ctx.enter_context(tc.psum_pool(name="psum_w", bufs=1))
         psum_acc = ctx.enter_context(tc.psum_pool(name="psum_acc", bufs=BLOCKS - 1))
         psum_last = ctx.enter_context(tc.psum_pool(name="psum_last", bufs=B))
@@ -36,13 +37,15 @@ def tile_nonoverlappingconv1d_shared_s_kernel(tc, x, weight, out):
         w_rows = keep.tile([O, B, C * TAPS], BF16)
         w_hbm = weight.rearrange("o c one k -> o (c one k)")
         x_rows = x.rearrange("b (q t) d -> (b q) t d", t=PACK)
+        half = BLOCK // 2
+        loads = [(0, BLOCK), (BLOCK, BLOCK), (2 * BLOCK, BLOCK)]
+        loads += [(3 * BLOCK, half), (3 * BLOCK + half, half)]
         raws = []
-        for block in range(BLOCKS):
-            start = block * BLOCK * SPAN
-            raw = stream.tile([PARTS, PACK, BLOCK * SPAN], BF16, name="raw")
-            nc.sync.dma_start(out=raw[:], in_=x_rows[:, :, start : start + BLOCK * SPAN])
+        for i, (first, n) in enumerate(loads):
+            raw = raw_pool.tile([PARTS, PACK, n * SPAN], BF16, name="raw")
+            nc.sync.dma_start(out=raw[:], in_=x_rows[:, :, first * SPAN : (first + n) * SPAN])
             raws.append(raw)
-            if block == 0:
+            if i == 0:
                 nc.sync.dma_start(out=w_rows[:, 0, :], in_=w_hbm)
 
         nc.scalar.copy(out=w_rows[:, 1, :], in_=w_rows[:, 0, :])
@@ -86,18 +89,20 @@ def tile_nonoverlappingconv1d_shared_s_kernel(tc, x, weight, out):
             codes.append(x_codes)
             scales.append(x_scales)
 
-        def sum_pairs(block, first, n):
-            pairs = raws[block][:].rearrange("q t (p k s) -> q p t k s", k=TAPS, s=PAIR)
+        def sum_pairs(i, first, n):
+            at = loads[i][0] + first
+            block, place = at // BLOCK, at % BLOCK
+            pairs = raws[i][:].rearrange("q t (p k s) -> q p t k s", k=TAPS, s=PAIR)
             target = grouped[block][:].rearrange("q k (p t) -> q p t k", t=PACK)
             nc.vector.tensor_tensor(
-                out=target[:, first : first + n],
+                out=target[:, place : place + n],
                 in0=pairs[:, first : first + n, :, :, 0],
                 in1=pairs[:, first : first + n, :, :, 1],
                 op=mybir.AluOpType.add,
             )
 
-        def split_words(block, first, n):
-            values = raws[block][:].rearrange("q t (p j) -> q p t j", j=SPAN)
+        def split_words(i, first, n):
+            values = raws[i][:].rearrange("q t (p j) -> q p t j", j=SPAN)
             apart = stream.tile([PARTS, SPAN, n * PACK], BF16, name="apart")
             nc.scalar.copy(
                 out=apart[:].rearrange("q j (p t) -> q p t j", t=PACK),
@@ -105,12 +110,14 @@ def tile_nonoverlappingconv1d_shared_s_kernel(tc, x, weight, out):
             )
             return apart
 
-        def sum_apart(block, first, n, apart):
+        def sum_apart(i, first, n, apart, taps):
+            at = loads[i][0] + first
+            block, place = at // BLOCK, at % BLOCK
             pairs = apart[:].rearrange("q (k s) m -> q k s m", s=PAIR)
             nc.vector.tensor_tensor(
-                out=grouped[block][:, :, first * PACK : (first + n) * PACK],
-                in0=pairs[:, :, 0, :],
-                in1=pairs[:, :, 1, :],
+                out=grouped[block][:, taps, place * PACK : (place + n) * PACK],
+                in0=pairs[:, taps, 0, :],
+                in1=pairs[:, taps, 1, :],
                 op=mybir.AluOpType.add,
             )
 
@@ -123,9 +130,8 @@ def tile_nonoverlappingconv1d_shared_s_kernel(tc, x, weight, out):
             )
 
         both = range(TAPS)
-        half = BLOCK // 2
         apart2 = split_words(2, half, half)
-        apart3 = split_words(3, half, half)
+        apart3 = split_words(3, 0, half)
         sum_pairs(0, 0, BLOCK)
         sum_pairs(1, 0, BLOCK)
         quantise(0, both)
@@ -133,13 +139,13 @@ def tile_nonoverlappingconv1d_shared_s_kernel(tc, x, weight, out):
         quantise(1, both)
         for b in range(B):
             quantise_weight(b)
-        sum_apart(2, half, half, apart2)
-        sum_pairs(3, 0, half)
-        quantise(2, range(0, 1))
-        sum_apart(3, half, half, apart3)
-        quantise(2, range(1, 2))
-        quantise(3, range(0, 1))
-        quantise(3, range(1, 2))
+        sum_pairs(4, 0, half)
+        sum_apart(2, half, half, apart2, slice(0, TAPS))
+        quantise(2, both)
+        for k in range(TAPS):
+            sum_apart(3, 0, half, apart3, slice(k, k + 1))
+        for k in range(TAPS):
+            quantise(3, range(k, k + 1))
 
         def multiply(acc, block, b, k):
             nc.tensor.matmul_mx(

@@ -17,6 +17,7 @@ POSITIONS = D // SPAN
 PARTS = 128
 PACK = 4
 HALF = C // PACK
+NEAR = 2
 BLOCK = 128
 BLOCKS = POSITIONS // BLOCK
 FLOPS = 2 * B * O * POSITIONS * C * TAPS
@@ -40,13 +41,12 @@ def tile_nonoverlappingconv1d_shared_s_kernel(tc, x, weight, out):
         half = BLOCK // 2
         loads = [(0, BLOCK), (BLOCK, BLOCK), (2 * BLOCK, BLOCK)]
         loads += [(3 * BLOCK, half), (3 * BLOCK + half, half)]
+        nc.sync.dma_start(out=w_rows[:, 0, :], in_=w_hbm)
         raws = []
         for i, (first, n) in enumerate(loads):
             raw = raw_pool.tile([PARTS, PACK, n * SPAN], BF16, name="raw")
             nc.sync.dma_start(out=raw[:], in_=x_rows[:, :, first * SPAN : (first + n) * SPAN])
             raws.append(raw)
-            if i == 0:
-                nc.sync.dma_start(out=w_rows[:, 0, :], in_=w_hbm)
 
         nc.scalar.copy(out=w_rows[:, 1, :], in_=w_rows[:, 0, :])
         identity = keep.tile([PARTS, PARTS], F32)
@@ -101,6 +101,15 @@ def tile_nonoverlappingconv1d_shared_s_kernel(tc, x, weight, out):
                 op=mybir.AluOpType.add,
             )
 
+        def sum_tap(i, k):
+            pairs = raws[i][:].rearrange("q t (g h k s) -> q k g t h s", h=NEAR, k=TAPS, s=PAIR)
+            nc.vector.tensor_tensor(
+                out=grouped[i][:, k, :].rearrange("q (g h t) -> q g t h", h=NEAR, t=PACK),
+                in0=pairs[:, k, :, :, :, 0],
+                in1=pairs[:, k, :, :, :, 1],
+                op=mybir.AluOpType.add,
+            )
+
         def split_words(i, first, n):
             values = raws[i][:].rearrange("q t (p j) -> q p t j", j=SPAN)
             apart = stream.tile([PARTS, SPAN, n * PACK], BF16, name="apart")
@@ -130,18 +139,23 @@ def tile_nonoverlappingconv1d_shared_s_kernel(tc, x, weight, out):
             )
 
         both = range(TAPS)
+        apart1 = split_words(1, half, half)
         apart2 = split_words(2, half, half)
         apart3 = split_words(3, 0, half)
-        sum_pairs(0, 0, BLOCK)
-        sum_pairs(1, 0, BLOCK)
-        quantise(0, both)
-        sum_pairs(2, 0, half)
-        quantise(1, both)
+        all_taps = slice(0, TAPS)
+        for k in range(TAPS):
+            sum_tap(0, k)
+        for k in range(TAPS):
+            quantise(0, range(k, k + 1))
+        sum_pairs(1, 0, half)
         for b in range(B):
             quantise_weight(b)
-        sum_pairs(4, 0, half)
-        sum_apart(2, half, half, apart2, slice(0, TAPS))
+        sum_pairs(2, 0, half)
+        sum_apart(1, half, half, apart1, all_taps)
+        sum_apart(2, half, half, apart2, all_taps)
+        quantise(1, both)
         quantise(2, both)
+        sum_pairs(4, 0, half)
         for k in range(TAPS):
             sum_apart(3, 0, half, apart3, slice(k, k + 1))
         for k in range(TAPS):

@@ -31,6 +31,7 @@ def tile_nonoverlappingconv1d_shared_s_kernel(tc, x, weight, out):
         keep = ctx.enter_context(tc.tile_pool(name="keep", bufs=1))
         stream = ctx.enter_context(tc.tile_pool(name="stream", bufs=BLOCKS))
         raw_pool = ctx.enter_context(tc.tile_pool(name="raw_pool", bufs=5))
+        psum_sum = ctx.enter_context(tc.psum_pool(name="psum_sum", bufs=1))
         psum_w = ctx.enter_context(tc.psum_pool(name="psum_w", bufs=1))
         psum_acc = ctx.enter_context(tc.psum_pool(name="psum_acc", bufs=BLOCKS - 1))
         psum_last = ctx.enter_context(tc.psum_pool(name="psum_last", bufs=B))
@@ -51,6 +52,8 @@ def tile_nonoverlappingconv1d_shared_s_kernel(tc, x, weight, out):
         nc.scalar.copy(out=w_rows[:, 1, :], in_=w_rows[:, 0, :])
         identity = keep.tile([PARTS, PARTS], F32)
         make_identity(nc, identity[:])
+        identity_bf16 = keep.tile([PARTS, PARTS], BF16)
+        make_identity(nc, identity_bf16[:])
         w_words = w_rows[:].rearrange("o b j -> o (b j)").bitcast(F32)
         w_turned = psum_w.tile([PARTS, PACK, O], F32)
         for t in range(PACK):
@@ -119,6 +122,26 @@ def tile_nonoverlappingconv1d_shared_s_kernel(tc, x, weight, out):
             )
             return apart
 
+        def sum_on_tensor(i, first, n):
+            pairs = raws[i][:].rearrange("q t (p k s) -> q s k p t", k=TAPS, s=PAIR)
+            sums = psum_sum.tile([PARTS, TAPS, n * PACK], F32, name="sums")
+            for s in range(PAIR):
+                nc.tensor.matmul(
+                    sums[:].rearrange("q k (p t) -> q k p t", t=PACK),
+                    lhsT=identity_bf16[:],
+                    rhs=pairs[:, s, :, first : first + n, :],
+                    start=(s == 0),
+                    stop=(s == PAIR - 1),
+                )
+            return sums
+
+        def round_sums(i, first, n, sums):
+            at = loads[i][0] + first
+            block, place = at // BLOCK, at % BLOCK
+            nc.scalar.copy(
+                out=grouped[block][:, :, place * PACK : (place + n) * PACK], in_=sums[:]
+            )
+
         def sum_apart(i, first, n, apart, taps):
             at = loads[i][0] + first
             block, place = at // BLOCK, at % BLOCK
@@ -140,7 +163,11 @@ def tile_nonoverlappingconv1d_shared_s_kernel(tc, x, weight, out):
 
         both = range(TAPS)
         apart1 = split_words(1, half, half)
-        apart2 = split_words(2, half, half)
+        quarter = half // 2
+        few = 24
+        sums2 = sum_on_tensor(2, 0, few)
+        apart2 = split_words(2, BLOCK - quarter, quarter)
+        round_sums(2, 0, few, sums2)
         apart3 = split_words(3, 0, half)
         all_taps = slice(0, TAPS)
         for k in range(TAPS):
@@ -150,9 +177,9 @@ def tile_nonoverlappingconv1d_shared_s_kernel(tc, x, weight, out):
         sum_pairs(1, 0, half)
         for b in range(B):
             quantise_weight(b)
-        sum_pairs(2, 0, half)
+        sum_pairs(2, few, BLOCK - quarter - few)
         sum_apart(1, half, half, apart1, all_taps)
-        sum_apart(2, half, half, apart2, all_taps)
+        sum_apart(2, BLOCK - quarter, quarter, apart2, all_taps)
         quantise(1, both)
         quantise(2, both)
         sum_pairs(4, 0, half)

from contextlib import ExitStack

import concourse.mybir as mybir
from concourse.masks import make_identity

BF16 = mybir.dt.bfloat16
F32 = mybir.dt.float32
U32 = mybir.dt.uint32
U8 = mybir.dt.uint8
FP8X4 = mybir.dt.float8_e4m3fn_x4

B, C, D, O = 2, 256, 2048, 128
TAPS = 2
PAIR = 2
SPAN = TAPS * PAIR
POSITIONS = D // SPAN
PARTS = 128
PACK = 4
HALF = C // PACK
NEAR = 2
BLOCK = 128
BLOCKS = POSITIONS // BLOCK
FLOPS = 2 * B * O * POSITIONS * C * TAPS


def tile_nonoverlappingconv1d_shared_s_kernel(tc, x, weight, out):
    nc = tc.nc

    with ExitStack() as ctx:
        ctx.enter_context(tc.manual_schedule())
        keep = ctx.enter_context(tc.tile_pool(name="keep", bufs=1))
        stream = ctx.enter_context(tc.tile_pool(name="stream", bufs=BLOCKS))
        raw_pool = ctx.enter_context(tc.tile_pool(name="raw_pool", bufs=5))
        psum_sum = ctx.enter_context(tc.psum_pool(name="psum_sum", bufs=1))
        psum_w = ctx.enter_context(tc.psum_pool(name="psum_w", bufs=1))
        psum_acc = ctx.enter_context(tc.psum_pool(name="psum_acc", bufs=BLOCKS - 1))
        psum_last = ctx.enter_context(tc.psum_pool(name="psum_last", bufs=B))

        w_rows = keep.tile([O, B, C * TAPS], BF16)
        w_hbm = weight.rearrange("o c one k -> o (c one k)")
        x_rows = x.rearrange("b (q t) d -> (b q) t d", t=PACK)
        half = BLOCK // 2
        loads = [(0, BLOCK), (BLOCK, BLOCK), (2 * BLOCK, BLOCK)]
        loads += [(3 * BLOCK, half), (3 * BLOCK + half, half)]
        nc.sync.dma_start(out=w_rows[:, 0, :], in_=w_hbm)
        raws = []
        for i, (first, n) in enumerate(loads):
            raw = raw_pool.tile([PARTS, PACK, n * SPAN], BF16, name="raw")
            nc.sync.dma_start(out=raw[:], in_=x_rows[:, :, first * SPAN : (first + n) * SPAN])
            raws.append(raw)

        nc.scalar.copy(out=w_rows[:, 1, :], in_=w_rows[:, 0, :])
        identity = keep.tile([PARTS, PARTS], F32)
        make_identity(nc, identity[:])
        identity_bf16 = keep.tile([PARTS, PARTS], BF16)
        make_identity(nc, identity_bf16[:])
        w_words = w_rows[:].rearrange("o b j -> o (b j)").bitcast(F32)
        w_turned = psum_w.tile([PARTS, PACK, O], F32)
        for t in range(PACK):
            nc.tensor.transpose(w_turned[:, t, :], w_words[:, t : B * C : PACK], identity[:])
        w_pairs = w_turned[:].rearrange("q t o -> q (t o)").bitcast(BF16)
        w_pairs = w_pairs.rearrange("q (t o k) -> q k o t", t=PACK, k=TAPS)
        w_grouped = keep.tile([PARTS, TAPS * O * PACK], BF16, align_bytes=64)
        nc.scalar.copy(
            out=w_grouped[:].rearrange("q (k o t) -> q k o t", k=TAPS, t=PACK), in_=w_pairs
        )
        w_codes = []
        w_scales = []
        for b in range(B):
            w_code = keep.tile([PARTS, TAPS, O], U32, align_bytes=64, name=f"w_codes{b}")
            w_scale = keep.tile([PARTS, TAPS, O], U8, align_bytes=64, name=f"w_scales{b}")
            w_codes.append(w_code)
            w_scales.append(w_scale)

        def quantise_weight(b):
            nc.vector.quantize_mx(
                out=w_codes[b][:].rearrange("q k o -> q (k o)").bitcast(FP8X4),
                scales=w_scales[b][:].rearrange("q k o -> q (k o)"),
                in_=w_grouped[:],
            )
            other = 1 - b
            nc.gpsimd.memset(w_codes[b][other * HALF : (other + 1) * HALF], 0)

        grouped = []
        codes = []
        scales = []
        for block in range(BLOCKS):
            x_grouped = stream.tile([PARTS, TAPS, BLOCK * PACK], BF16, align_bytes=64, name="x_grouped")
            x_codes = stream.tile([PARTS, TAPS, BLOCK], U32, align_bytes=64, name="x_codes")
            x_scales = stream.tile([PARTS, TAPS, BLOCK], U8, align_bytes=64, name="x_scales")
            grouped.append(x_grouped)
            codes.append(x_codes)
            scales.append(x_scales)

        def sum_pairs(i, first, n):
            at = loads[i][0] + first
            block, place = at // BLOCK, at % BLOCK
            pairs = raws[i][:].rearrange("q t (p k s) -> q p t k s", k=TAPS, s=PAIR)
            target = grouped[block][:].rearrange("q k (p t) -> q p t k", t=PACK)
            nc.vector.tensor_tensor(
                out=target[:, place : place + n],
                in0=pairs[:, first : first + n, :, :, 0],
                in1=pairs[:, first : first + n, :, :, 1],
                op=mybir.AluOpType.add,
            )

        def sum_tap(i, k):
            pairs = raws[i][:].rearrange("q t (g h k s) -> q k g t h s", h=NEAR, k=TAPS, s=PAIR)
            nc.vector.tensor_tensor(
                out=grouped[i][:, k, :].rearrange("q (g h t) -> q g t h", h=NEAR, t=PACK),
                in0=pairs[:, k, :, :, :, 0],
                in1=pairs[:, k, :, :, :, 1],
                op=mybir.AluOpType.add,
            )

        def split_words(i, first, n):
            values = raws[i][:].rearrange("q t (p j) -> q p t j", j=SPAN)
            apart = stream.tile([PARTS, SPAN, n * PACK], BF16, name="apart")
            nc.scalar.copy(
                out=apart[:].rearrange("q j (p t) -> q p t j", t=PACK),
                in_=values[:, first : first + n],
            )
            return apart

        def sum_on_tensor(i, first, n):
            pairs = raws[i][:].rearrange("q t (p k s) -> q s k p t", k=TAPS, s=PAIR)
            sums = psum_sum.tile([PARTS, TAPS, n * PACK], F32, name="sums")
            for s in range(PAIR):
                nc.tensor.matmul(
                    sums[:].rearrange("q k (p t) -> q k p t", t=PACK),
                    lhsT=identity_bf16[:],
                    rhs=pairs[:, s, :, first : first + n, :],
                    start=(s == 0),
                    stop=(s == PAIR - 1),
                )
            return sums

        def round_sums(i, first, n, sums):
            at = loads[i][0] + first
            block, place = at // BLOCK, at % BLOCK
            nc.scalar.copy(
                out=grouped[block][:, :, place * PACK : (place + n) * PACK], in_=sums[:]
            )

        def sum_apart(i, first, n, apart, taps):
            at = loads[i][0] + first
            block, place = at // BLOCK, at % BLOCK
            pairs = apart[:].rearrange("q (k s) m -> q k s m", s=PAIR)
            nc.vector.tensor_tensor(
                out=grouped[block][:, taps, place * PACK : (place + n) * PACK],
                in0=pairs[:, taps, 0, :],
                in1=pairs[:, taps, 1, :],
                op=mybir.AluOpType.add,
            )

        def quantise(block, taps):
            taps = slice(taps[0], taps[-1] + 1)
            nc.vector.quantize_mx(
                out=codes[block][:, taps, :].rearrange("q k p -> q (k p)").bitcast(FP8X4),
                scales=scales[block][:, taps, :].rearrange("q k p -> q (k p)"),
                in_=grouped[block][:, taps, :].rearrange("q k j -> q (k j)"),
            )

        both = range(TAPS)
        apart1 = split_words(1, half, half)
        quarter = half // 2
        few = 24
        sums2 = sum_on_tensor(2, 0, few)
        apart2 = split_words(2, BLOCK - quarter, quarter)
        round_sums(2, 0, few, sums2)
        apart3 = split_words(3, 0, half)
        all_taps = slice(0, TAPS)
        for k in range(TAPS):
            sum_tap(0, k)
        for k in range(TAPS):
            quantise(0, range(k, k + 1))
        sum_pairs(1, 0, half)
        for b in range(B):
            quantise_weight(b)
        sum_pairs(2, few, BLOCK - quarter - few)
        sum_apart(1, half, half, apart1, all_taps)
        sum_apart(2, BLOCK - quarter, quarter, apart2, all_taps)
        quantise(1, both)
        quantise(2, both)
        sum_pairs(4, 0, half)
        for k in range(TAPS):
            sum_apart(3, 0, half, apart3, slice(k, k + 1))
        for k in range(TAPS):
            quantise(3, range(k, k + 1))

        def multiply(acc, block, b, k):
            nc.tensor.matmul_mx(
                out=acc,
                lhsT=w_codes[b][:, k, :].bitcast(FP8X4),
                lhsT_scale=w_scales[b][:, k, :],
                rhs=codes[block][:, k, :].bitcast(FP8X4),
                rhs_scale=scales[block][:, k, :],
                start=(k == 0),
                stop=(k == TAPS - 1),
            )

        out_rows = out.rearrange("b o p -> o b p")
        for block in range(BLOCKS - 1):
            acc = psum_acc.tile([O, B, BLOCK], F32, name="acc")
            for b in range(B):
                for k in range(TAPS):
                    multiply(acc[:, b, :], block, b, k)
            result = stream.tile([O, B, BLOCK], F32, name="result")
            nc.scalar.mul(out=result[:], in_=acc[:], mul=1.0 / 16.0)
            nc.sync.dma_start(
                out=out_rows[:, :, block * BLOCK : (block + 1) * BLOCK], in_=result[:]
            )

        last = BLOCKS - 1
        accs = []
        for b in range(B):
            acc_last = psum_last.tile([O, BLOCK], F32, name="acc_last")
            accs.append(acc_last)
        for k in range(TAPS):
            for b in range(B):
                multiply(accs[b][:], last, b, k)
        columns = slice(last * BLOCK, (last + 1) * BLOCK)
        result0 = keep.tile([O, BLOCK], F32)
        nc.scalar.mul(out=result0[:], in_=accs[0][:], mul=1.0 / 16.0)
        nc.sync.dma_start(out=out[0, :, columns], in_=result0[:])
        result1 = keep.tile([O, BLOCK], F32)
        nc.vector.tensor_scalar_mul(result1[:], accs[1][:], 1.0 / 16.0)
        nc.scalar.dma_start(out=out[1, :, columns], in_=result1[:])
